import numpy as np
import ml_dtypes


def mxq(x, axis, fmt="e4m3"):
    dtype, down = {"e4m3": (ml_dtypes.float8_e4m3fn, 7), "e5m2": (ml_dtypes.float8_e5m2, 14)}[fmt]
    v = np.moveaxis(np.asarray(x, np.float32).astype(ml_dtypes.bfloat16).astype(np.float64), axis, -1)
    blocks = v.reshape(v.shape[:-1] + (-1, 32))
    amax = np.abs(blocks).max(-1, keepdims=True)
    byte = np.maximum(np.where(amax > 0, np.frexp(amax)[1] - 1 + 127, 0) - down, 1)
    scale = np.exp2(byte - 127.0)
    codes = (blocks / scale).astype(np.float32).astype(dtype).astype(np.float64)
    return np.moveaxis((codes * scale).reshape(v.shape), -1, axis)


WIDE = False


def mx_kscale(k):
    if not WIDE:
        return np.ones(k)
    levels = np.array([10, -10, 5, -5, 0])
    a = np.random.permutation(np.resize(levels, k // 512 * 4)).reshape(k // 512, 4)
    idx = np.arange(k)
    return np.exp2(a[idx // 512, idx % 128 // 32])


BF16 = ml_dtypes.bfloat16


def bf(x):
    return np.asarray(x, np.float32).astype(BF16)


def f64(x):
    return np.asarray(x).astype(np.float64)


B, DIM, D2, T = 1, 512, 1024, 512


def setup_inputs():
    s = mx_kscale(D2)
    es = 0.25 * s[None, :, None]
    ws = 0.35 / np.sqrt(D2) / s[:, None] / s[None, :]
    return {"E_re": bf(np.random.standard_normal((B, D2, T)) * es),
            "E_im": bf(np.random.standard_normal((B, D2, T)) * es),
            "WKQ_re": bf(np.random.standard_normal((D2, D2)) * ws),
            "WKQ_im": bf(np.random.standard_normal((D2, D2)) * ws)}


def reference(E_re, E_im, WKQ_re, WKQ_im):
    er = mxq(f64(E_re), 1, "e4m3")
    ei = mxq(f64(E_im), 1, "e4m3")
    wr = mxq(f64(WKQ_re), 1, "e4m3")
    wi = mxq(f64(WKQ_im), 1, "e4m3")
    q_re = (wr @ er) - (wi @ ei)
    q_im = (wr @ ei) + (wi @ er)
    qr = mxq(q_re, 1, "e4m3")
    qi = mxq(q_im, 1, "e4m3")
    ert = er.transpose(0, 2, 1)
    eit = ei.transpose(0, 2, 1)
    s_re = (ert @ qr) + (eit @ qi)
    s_im = (ert @ qi) - (eit @ qr)
    return s_re, s_im

@@ -1,0 +1,203 @@
+from contextlib import ExitStack
+
+import concourse.mybir as mybir
+from concourse.masks import make_identity
+
+BF16 = mybir.dt.bfloat16
+F32 = mybir.dt.float32
+U32 = mybir.dt.uint32
+U8 = mybir.dt.uint8
+FP8X4 = mybir.dt.float8_e4m3fn_x4
+
+P = 128
+PACK = 4
+CHANNELS = 1024
+POSITIONS = 512
+PASSES = CHANNELS // (P * PACK)
+BANK = 512
+PAIRS = CHANNELS // (2 * P)
+POSITION_TILES = POSITIONS // P
+
+FLOPS = 2 * 4 * CHANNELS * CHANNELS * POSITIONS + 2 * 4 * POSITIONS * CHANNELS * POSITIONS
+
+STAGE1_E = {"re": ("re", "neg"), "im": ("im", "re")}
+STAGE2_TERMS = {"re": (("re", "re"), ("im", "im")), "im": (("re", "im"), ("neg", "re"))}
+
+
+def regroup(nc, grouped, rows):
+    nc.vector.tensor_copy(
+        out=grouped.rearrange("p (c i j) -> p c j i", i=4, j=PACK),
+        in_=rows.rearrange("p j (c i) -> p c j i", i=4),
+    )
+
+
+def tile_autoregressivelsa_pa_kernel(tc, E_re, E_im, WKQ_re, WKQ_im, out_0, out_1):
+    nc = tc.nc
+    e_dram = {"re": E_re, "im": E_im}
+    w_dram = {"re": WKQ_re, "im": WKQ_im}
+    s_dram = {"re": out_0, "im": out_1}
+
+    with ExitStack() as ctx:
+        keep = ctx.enter_context(tc.tile_pool(name="keep", bufs=1))
+        left_banks = ctx.enter_context(tc.psum_pool(name="left_banks", bufs=4))
+        right_banks = ctx.enter_context(tc.psum_pool(name="right_banks", bufs=4))
+        ctx.enter_context(tc.manual_schedule())
+
+        identity = keep.tile([P, P], F32, name="identity")
+        make_identity(nc, identity[:])
+
+        e_raw = {}
+        for x in ("re", "im"):
+            e_raw[x] = keep.tile([P, PASSES, PACK, POSITIONS], BF16, name="e_raw_" + x)
+        e_codes = {}
+        e_scales = {}
+        for x in ("re", "im", "neg"):
+            e_codes[x] = keep.tile([P, PASSES, POSITIONS], U32, name="e_codes_" + x, align_bytes=64)
+            e_scales[x] = keep.tile([P, PASSES, POSITIONS], U8, name="e_scales_" + x, align_bytes=64)
+        w_raw = {}
+        for q in range(PAIRS):
+            for x in ("re", "im"):
+                w_raw[(x, q)] = keep.tile([P, 2 * CHANNELS], BF16, name="w_raw_%s%d" % (x, q))
+        w_codes = keep.tile([P, PAIRS, 2, 2 * PASSES * P], U32, name="w_codes", align_bytes=64)
+        w_scales = keep.tile([P, PAIRS, 2, 2 * PASSES * P], U8, name="w_scales", align_bytes=64)
+        q_raw = {}
+        q_codes = {}
+        q_scales = {}
+        for part in ("re", "im"):
+            q_raw[part] = keep.tile([P, PAIRS, 2, POSITIONS], BF16, name="q_raw_" + part)
+            q_codes[part] = keep.tile([P, PASSES, POSITIONS], U32, name="q_codes_" + part, align_bytes=64)
+            q_scales[part] = keep.tile([P, PASSES, POSITIONS], U8, name="q_scales_" + part, align_bytes=64)
+
+        def load_e(g):
+            for x in ("re", "im"):
+                nc.sync.dma_start(
+                    out=e_raw[x][:, g, :, :].rearrange("p (u e) t -> p u (e t)", u=2, e=2),
+                    in_=e_dram[x].rearrange("b (g u p e) t -> b g p u (e t)", g=PASSES, u=2, p=P, e=2)[
+                        0, g, :, :, :
+                    ],
+                )
+
+        def load_w(q):
+            for x in ("re", "im"):
+                nc.sync.dma_start(
+                    out=w_raw[(x, q)][:],
+                    in_=w_dram[x].rearrange("(q p e) c -> q p (e c)", q=PAIRS, p=P, e=2)[q, :, :],
+                )
+
+        load_e(0)
+        load_w(0)
+        load_e(1)
+        for q in range(1, PAIRS):
+            load_w(q)
+
+        def quantise_e(g):
+            grouped = {}
+            for x in ("re", "im", "neg"):
+                grouped[x] = keep.tile([P, PACK * POSITIONS], BF16, name="e_grp_%s%d" % (x, g), align_bytes=64)
+            regroup(nc, grouped["re"][:], e_raw["re"][:, g, :, :])
+            regroup(nc, grouped["im"][:], e_raw["im"][:, g, :, :])
+            for x in ("re", "im", "neg"):
+                if x == "neg":
+                    nc.vector.tensor_scalar_mul(out=grouped["neg"][:], in0=grouped["im"][:], scalar1=-1.0)
+                nc.vector.quantize_mx(
+                    out=e_codes[x][:, g, :].bitcast(FP8X4), scales=e_scales[x][:, g, :], in_=grouped[x][:]
+                )
+
+        def transpose_w(q):
+            grouped = []
+            for e in range(2):
+                words_out = keep.tile([P, 2 * BANK], F32, name="w_grp_%d%d" % (q, e), align_bytes=64)
+                grouped.append(words_out)
+                for xi, x in enumerate(("re", "im")):
+                    words_in = w_raw[(x, q)][:].bitcast(F32)
+                    bank = left_banks.tile([P, BANK], F32, name="w_bank", tag="left")
+                    for gu in range(PASSES * 2):
+                        nc.tensor.transpose(
+                            bank[:, gu * P : (gu + 1) * P],
+                            words_in[:, e * BANK + gu * P : e * BANK + (gu + 1) * P],
+                            identity[:],
+                        )
+                    nc.scalar.copy(
+                        out=words_out[:, xi * BANK : (xi + 1) * BANK].rearrange(
+                            "p (g m u) -> p g m u", g=PASSES, m=P, u=2
+                        ),
+                        in_=bank[:].rearrange("p (g u m) -> p g m u", g=PASSES, u=2, m=P),
+                    )
+            return grouped
+
+        def quantise_w(q, grouped):
+            for e in range(2):
+                nc.vector.quantize_mx(
+                    out=w_codes[:, q, e, :].bitcast(FP8X4),
+                    scales=w_scales[:, q, e, :],
+                    in_=grouped[e][:].bitcast(BF16),
+                )
+
+        def stage1_passes(q, g, q_acc):
+            for e in range(2):
+                for part in ("im", "re"):
+                    for xi, operand in enumerate(STAGE1_E[part]):
+                        w_cols = slice((xi * PASSES + g) * P, (xi * PASSES + g + 1) * P)
+                        nc.tensor.matmul_mx(
+                            out=q_acc[(e, part)][:],
+                            lhsT=w_codes[:, q, e, w_cols].bitcast(FP8X4),
+                            lhsT_scale=w_scales[:, q, e, w_cols],
+                            rhs=e_codes[operand][:, g, :].bitcast(FP8X4),
+                            rhs_scale=e_scales[operand][:, g, :],
+                            start=(g == 0 and xi == 0),
+                            stop=(g == PASSES - 1 and xi == 1),
+                        )
+                    if g == PASSES - 1:
+                        nc.scalar.copy(out=q_raw[part][:, q, e, :], in_=q_acc[(e, part)][:])
+
+        def quantise_q(g):
+            grouped = {}
+            for part in ("re", "im"):
+                grouped[part] = keep.tile([P, PACK * POSITIONS], BF16, name="q_grp_%s%d" % (part, g), align_bytes=64)
+                regroup(nc, grouped[part][:], q_raw[part][:, 2 * g : 2 * g + 2, :, :].rearrange("p u e t -> p (u e) t"))
+            for part in ("re", "im"):
+                nc.vector.quantize_mx(
+                    out=q_codes[part][:, g, :].bitcast(FP8X4), scales=q_scales[part][:, g, :], in_=grouped[part][:]
+                )
+
+        quantise_e(0)
+        quantise_w(0, transpose_w(0))
+        quantise_e(1)
+        for q in range(PAIRS):
+            q_acc = {}
+            for e in range(2):
+                for part in ("im", "re"):
+                    q_acc[(e, part)] = right_banks.tile([P, BANK], F32, name="q_acc", tag="right")
+            stage1_passes(q, 0, q_acc)
+            if q + 1 < PAIRS:
+                quantise_w(q + 1, transpose_w(q + 1))
+            stage1_passes(q, 1, q_acc)
+            if q % 2 == 1:
+                quantise_q(q // 2)
+
+        s_banks = {"re": (left_banks, "left"), "im": (right_banks, "right")}
+        s_acc = {}
+        for g in range(PASSES):
+            for part in ("re", "im"):
+                for i in range(POSITION_TILES):
+                    if g == 0:
+                        pool, tag = s_banks[part]
+                        s_acc[(part, i)] = pool.tile([P, BANK], F32, name="s_acc", tag=tag)
+                    rows = slice(i * P, (i + 1) * P)
+                    for n, (operand, q_part) in enumerate(STAGE2_TERMS[part]):
+                        nc.tensor.matmul_mx(
+                            out=s_acc[(part, i)][:],
+                            lhsT=e_codes[operand][:, g, rows].bitcast(FP8X4),
+                            lhsT_scale=e_scales[operand][:, g, rows],
+                            rhs=q_codes[q_part][:, g, :].bitcast(FP8X4),
+                            rhs_scale=q_scales[q_part][:, g, :],
+                            start=(g == 0 and n == 0),
+                            stop=(g == PASSES - 1 and n == 1),
+                        )
+                    if g == PASSES - 1:
+                        s_sb = keep.tile([P, POSITIONS], F32, name="s_sb_%s%d" % (part, i))
+                        if i % 2 == 0:
+                            nc.scalar.copy(out=s_sb[:], in_=s_acc[(part, i)][:])
+                        else:
+                            nc.vector.tensor_copy(out=s_sb[:], in_=s_acc[(part, i)][:])
+                        nc.sync.dma_start(out=s_dram[part][0, rows, :], in_=s_sb[:])

@@ -17,6 +17,7 @@ PASSES = CHANNELS // (P * PACK)
 BANK = 512
 PAIRS = CHANNELS // (2 * P)
 POSITION_TILES = POSITIONS // P
+VECTOR_POSITIONS = 352
 
 FLOPS = 2 * 4 * CHANNELS * CHANNELS * POSITIONS + 2 * 4 * POSITIONS * CHANNELS * POSITIONS
 
@@ -24,10 +25,10 @@ STAGE1_E = {"re": ("re", "neg"), "im": ("im", "re")}
 STAGE2_TERMS = {"re": (("re", "re"), ("im", "im")), "im": (("re", "im"), ("neg", "re"))}
 
 
-def regroup(nc, grouped, rows):
-    nc.vector.tensor_copy(
-        out=grouped.rearrange("p (c i j) -> p c j i", i=4, j=PACK),
-        in_=rows.rearrange("p j (c i) -> p c j i", i=4),
+def regroup(engine_copy, grouped, rows, first, last):
+    engine_copy(
+        out=grouped.rearrange("p (c i j) -> p c j i", i=4, j=PACK)[:, first // 4 : last // 4, :, :],
+        in_=rows.rearrange("p j (c i) -> p c j i", i=4)[:, first // 4 : last // 4, :, :],
     )
 
 
@@ -57,7 +58,7 @@ def tile_autoregressivelsa_pa_kernel(tc, E_re, E_im, WKQ_re, WKQ_im, out_0, out_
         w_raw = {}
         for q in range(PAIRS):
             for x in ("re", "im"):
-                w_raw[(x, q)] = keep.tile([P, 2 * CHANNELS], BF16, name="w_raw_%s%d" % (x, q))
+                w_raw[(x, q)] = keep.tile([P, 2, CHANNELS], BF16, name="w_raw_%s%d" % (x, q))
         w_codes = keep.tile([P, PAIRS, 2, 2 * PASSES * P], U32, name="w_codes", align_bytes=64)
         w_scales = keep.tile([P, PAIRS, 2, 2 * PASSES * P], U8, name="w_scales", align_bytes=64)
         q_raw = {}
@@ -78,11 +79,12 @@ def tile_autoregressivelsa_pa_kernel(tc, E_re, E_im, WKQ_re, WKQ_im, out_0, out_
                 )
 
         def load_w(q):
-            for x in ("re", "im"):
-                nc.sync.dma_start(
-                    out=w_raw[(x, q)][:],
-                    in_=w_dram[x].rearrange("(q p e) c -> q p (e c)", q=PAIRS, p=P, e=2)[q, :, :],
-                )
+            for e in range(2):
+                for x in ("re", "im"):
+                    nc.sync.dma_start(
+                        out=w_raw[(x, q)][:, e, :],
+                        in_=w_dram[x].rearrange("(q p e) c -> q e p c", q=PAIRS, p=P, e=2)[q, e, :, :],
+                    )
 
         load_e(0)
         load_w(0)
@@ -90,18 +92,25 @@ def tile_autoregressivelsa_pa_kernel(tc, E_re, E_im, WKQ_re, WKQ_im, out_0, out_
         for q in range(1, PAIRS):
             load_w(q)
 
-        def quantise_e(g):
-            grouped = {}
+        e_grouped = {}
+        for g in range(PASSES):
             for x in ("re", "im", "neg"):
-                grouped[x] = keep.tile([P, PACK * POSITIONS], BF16, name="e_grp_%s%d" % (x, g), align_bytes=64)
-            regroup(nc, grouped["re"][:], e_raw["re"][:, g, :, :])
-            regroup(nc, grouped["im"][:], e_raw["im"][:, g, :, :])
-            for x in ("re", "im", "neg"):
-                if x == "neg":
-                    nc.vector.tensor_scalar_mul(out=grouped["neg"][:], in0=grouped["im"][:], scalar1=-1.0)
-                nc.vector.quantize_mx(
-                    out=e_codes[x][:, g, :].bitcast(FP8X4), scales=e_scales[x][:, g, :], in_=grouped[x][:]
+                e_grouped[(x, g)] = keep.tile(
+                    [P, PACK * POSITIONS], BF16, name="e_grp_%s%d" % (x, g), align_bytes=64
                 )
+
+        def quantise_e(x, g):
+            nc.vector.quantize_mx(
+                out=e_codes[x][:, g, :].bitcast(FP8X4), scales=e_scales[x][:, g, :], in_=e_grouped[(x, g)][:]
+            )
+
+        def prepare_e(g):
+            for x in ("re", "im"):
+                regroup(nc.vector.tensor_copy, e_grouped[(x, g)][:], e_raw[x][:, g, :, :], 0, VECTOR_POSITIONS)
+                regroup(nc.scalar.copy, e_grouped[(x, g)][:], e_raw[x][:, g, :, :], VECTOR_POSITIONS, POSITIONS)
+            quantise_e("re", g)
+            nc.vector.tensor_scalar_mul(out=e_grouped[("neg", g)][:], in0=e_grouped[("im", g)][:], scalar1=-1.0)
+            quantise_e("im", g)
 
         def transpose_w(q):
             grouped = []
@@ -109,12 +118,12 @@ def tile_autoregressivelsa_pa_kernel(tc, E_re, E_im, WKQ_re, WKQ_im, out_0, out_
                 words_out = keep.tile([P, 2 * BANK], F32, name="w_grp_%d%d" % (q, e), align_bytes=64)
                 grouped.append(words_out)
                 for xi, x in enumerate(("re", "im")):
-                    words_in = w_raw[(x, q)][:].bitcast(F32)
+                    words_in = w_raw[(x, q)][:, e, :].bitcast(F32)
                     bank = left_banks.tile([P, BANK], F32, name="w_bank", tag="left")
                     for gu in range(PASSES * 2):
                         nc.tensor.transpose(
                             bank[:, gu * P : (gu + 1) * P],
-                            words_in[:, e * BANK + gu * P : e * BANK + (gu + 1) * P],
+                            words_in[:, gu * P : (gu + 1) * P],
                             identity[:],
                         )
                     nc.scalar.copy(
@@ -125,17 +134,16 @@ def tile_autoregressivelsa_pa_kernel(tc, E_re, E_im, WKQ_re, WKQ_im, out_0, out_
                     )
             return grouped
 
-        def quantise_w(q, grouped):
-            for e in range(2):
-                nc.vector.quantize_mx(
-                    out=w_codes[:, q, e, :].bitcast(FP8X4),
-                    scales=w_scales[:, q, e, :],
-                    in_=grouped[e][:].bitcast(BF16),
-                )
+        def quantise_w(q, e, grouped):
+            nc.vector.quantize_mx(
+                out=w_codes[:, q, e, :].bitcast(FP8X4),
+                scales=w_scales[:, q, e, :],
+                in_=grouped[e][:].bitcast(BF16),
+            )
 
         def stage1_passes(q, g, q_acc):
-            for e in range(2):
-                for part in ("im", "re"):
+            for part in ("im", "re"):
+                for e in range(2):
                     for xi, operand in enumerate(STAGE1_E[part]):
                         w_cols = slice((xi * PASSES + g) * P, (xi * PASSES + g + 1) * P)
                         nc.tensor.matmul_mx(
@@ -151,26 +159,31 @@ def tile_autoregressivelsa_pa_kernel(tc, E_re, E_im, WKQ_re, WKQ_im, out_0, out_
                         nc.scalar.copy(out=q_raw[part][:, q, e, :], in_=q_acc[(e, part)][:])
 
         def quantise_q(g):
-            grouped = {}
-            for part in ("re", "im"):
-                grouped[part] = keep.tile([P, PACK * POSITIONS], BF16, name="q_grp_%s%d" % (part, g), align_bytes=64)
-                regroup(nc, grouped[part][:], q_raw[part][:, 2 * g : 2 * g + 2, :, :].rearrange("p u e t -> p (u e) t"))
-            for part in ("re", "im"):
+            for part in ("im", "re"):
+                grouped = keep.tile([P, PACK * POSITIONS], BF16, name="q_grp_%s%d" % (part, g), align_bytes=64)
+                rows = q_raw[part][:, 2 * g : 2 * g + 2, :, :].rearrange("p u e t -> p (u e) t")
+                regroup(nc.vector.tensor_copy, grouped[:], rows, 0, POSITIONS)
                 nc.vector.quantize_mx(
-                    out=q_codes[part][:, g, :].bitcast(FP8X4), scales=q_scales[part][:, g, :], in_=grouped[part][:]
+                    out=q_codes[part][:, g, :].bitcast(FP8X4), scales=q_scales[part][:, g, :], in_=grouped[:]
                 )
 
-        quantise_e(0)
-        quantise_w(0, transpose_w(0))
-        quantise_e(1)
+        prepare_e(0)
+        w_grouped = transpose_w(0)
+        quantise_w(0, 0, w_grouped)
+        quantise_e("neg", 0)
+        quantise_w(0, 1, w_grouped)
+        prepare_e(1)
+        quantise_e("neg", 1)
         for q in range(PAIRS):
             q_acc = {}
-            for e in range(2):
-                for part in ("im", "re"):
+            for part in ("im", "re"):
+                for e in range(2):
                     q_acc[(e, part)] = right_banks.tile([P, BANK], F32, name="q_acc", tag="right")
             stage1_passes(q, 0, q_acc)
             if q + 1 < PAIRS:
-                quantise_w(q + 1, transpose_w(q + 1))
+                w_grouped = transpose_w(q + 1)
+                quantise_w(q + 1, 0, w_grouped)
+                quantise_w(q + 1, 1, w_grouped)
             stage1_passes(q, 1, q_acc)
             if q % 2 == 1:
                 quantise_q(q // 2)

@@ -141,22 +141,21 @@ def tile_autoregressivelsa_pa_kernel(tc, E_re, E_im, WKQ_re, WKQ_im, out_0, out_
                 in_=grouped[e][:].bitcast(BF16),
             )
 
-        def stage1_passes(q, g, q_acc):
-            for part in ("im", "re"):
-                for e in range(2):
-                    for xi, operand in enumerate(STAGE1_E[part]):
-                        w_cols = slice((xi * PASSES + g) * P, (xi * PASSES + g + 1) * P)
-                        nc.tensor.matmul_mx(
-                            out=q_acc[(e, part)][:],
-                            lhsT=w_codes[:, q, e, w_cols].bitcast(FP8X4),
-                            lhsT_scale=w_scales[:, q, e, w_cols],
-                            rhs=e_codes[operand][:, g, :].bitcast(FP8X4),
-                            rhs_scale=e_scales[operand][:, g, :],
-                            start=(g == 0 and xi == 0),
-                            stop=(g == PASSES - 1 and xi == 1),
-                        )
-                    if g == PASSES - 1:
-                        nc.scalar.copy(out=q_raw[part][:, q, e, :], in_=q_acc[(e, part)][:])
+        def stage1_passes(q, g, part, q_acc):
+            for e in range(2):
+                for xi, operand in enumerate(STAGE1_E[part]):
+                    w_cols = slice((xi * PASSES + g) * P, (xi * PASSES + g + 1) * P)
+                    nc.tensor.matmul_mx(
+                        out=q_acc[(e, part)][:],
+                        lhsT=w_codes[:, q, e, w_cols].bitcast(FP8X4),
+                        lhsT_scale=w_scales[:, q, e, w_cols],
+                        rhs=e_codes[operand][:, g, :].bitcast(FP8X4),
+                        rhs_scale=e_scales[operand][:, g, :],
+                        start=(g == 0 and xi == 0),
+                        stop=(g == PASSES - 1 and xi == 1),
+                    )
+                if g == PASSES - 1:
+                    nc.scalar.copy(out=q_raw[part][:, q, e, :], in_=q_acc[(e, part)][:])
 
         def quantise_q(g):
             for part in ("im", "re"):
@@ -179,12 +178,14 @@ def tile_autoregressivelsa_pa_kernel(tc, E_re, E_im, WKQ_re, WKQ_im, out_0, out_
             for part in ("im", "re"):
                 for e in range(2):
                     q_acc[(e, part)] = right_banks.tile([P, BANK], F32, name="q_acc", tag="right")
-            stage1_passes(q, 0, q_acc)
+            stage1_passes(q, 0, "im", q_acc)
             if q + 1 < PAIRS:
                 w_grouped = transpose_w(q + 1)
                 quantise_w(q + 1, 0, w_grouped)
                 quantise_w(q + 1, 1, w_grouped)
-            stage1_passes(q, 1, q_acc)
+            stage1_passes(q, 0, "re", q_acc)
+            stage1_passes(q, 1, "im", q_acc)
+            stage1_passes(q, 1, "re", q_acc)
             if q % 2 == 1:
                 quantise_q(q // 2)
 

from contextlib import ExitStack

import concourse.mybir as mybir
from concourse.masks import make_identity

BF16 = mybir.dt.bfloat16
F32 = mybir.dt.float32
U32 = mybir.dt.uint32
U8 = mybir.dt.uint8
FP8X4 = mybir.dt.float8_e4m3fn_x4

P = 128
PACK = 4
CHANNELS = 1024
POSITIONS = 512
PASSES = CHANNELS // (P * PACK)
BANK = 512
PAIRS = CHANNELS // (2 * P)
POSITION_TILES = POSITIONS // P
VECTOR_POSITIONS = 352

FLOPS = 2 * 4 * CHANNELS * CHANNELS * POSITIONS + 2 * 4 * POSITIONS * CHANNELS * POSITIONS

STAGE1_E = {"re": ("re", "neg"), "im": ("im", "re")}
STAGE2_TERMS = {"re": (("re", "re"), ("im", "im")), "im": (("re", "im"), ("neg", "re"))}


def regroup(engine_copy, grouped, rows, first, last):
    engine_copy(
        out=grouped.rearrange("p (c i j) -> p c j i", i=4, j=PACK)[:, first // 4 : last // 4, :, :],
        in_=rows.rearrange("p j (c i) -> p c j i", i=4)[:, first // 4 : last // 4, :, :],
    )


def tile_autoregressivelsa_pa_kernel(tc, E_re, E_im, WKQ_re, WKQ_im, out_0, out_1):
    nc = tc.nc
    e_dram = {"re": E_re, "im": E_im}
    w_dram = {"re": WKQ_re, "im": WKQ_im}
    s_dram = {"re": out_0, "im": out_1}

    with ExitStack() as ctx:
        keep = ctx.enter_context(tc.tile_pool(name="keep", bufs=1))
        left_banks = ctx.enter_context(tc.psum_pool(name="left_banks", bufs=4))
        right_banks = ctx.enter_context(tc.psum_pool(name="right_banks", bufs=4))
        ctx.enter_context(tc.manual_schedule())

        identity = keep.tile([P, P], F32, name="identity")
        make_identity(nc, identity[:])

        e_raw = {}
        for x in ("re", "im"):
            e_raw[x] = keep.tile([P, PASSES, PACK, POSITIONS], BF16, name="e_raw_" + x)
        e_codes = {}
        e_scales = {}
        for x in ("re", "im", "neg"):
            e_codes[x] = keep.tile([P, PASSES, POSITIONS], U32, name="e_codes_" + x, align_bytes=64)
            e_scales[x] = keep.tile([P, PASSES, POSITIONS], U8, name="e_scales_" + x, align_bytes=64)
        w_raw = {}
        for q in range(PAIRS):
            for x in ("re", "im"):
                w_raw[(x, q)] = keep.tile([P, 2, CHANNELS], BF16, name="w_raw_%s%d" % (x, q))
        w_codes = keep.tile([P, PAIRS, 2, 2 * PASSES * P], U32, name="w_codes", align_bytes=64)
        w_scales = keep.tile([P, PAIRS, 2, 2 * PASSES * P], U8, name="w_scales", align_bytes=64)
        q_raw = {}
        q_codes = {}
        q_scales = {}
        for part in ("re", "im"):
            q_raw[part] = keep.tile([P, PAIRS, 2, POSITIONS], BF16, name="q_raw_" + part)
            q_codes[part] = keep.tile([P, PASSES, POSITIONS], U32, name="q_codes_" + part, align_bytes=64)
            q_scales[part] = keep.tile([P, PASSES, POSITIONS], U8, name="q_scales_" + part, align_bytes=64)

        def load_e(g):
            for x in ("re", "im"):
                nc.sync.dma_start(
                    out=e_raw[x][:, g, :, :].rearrange("p (u e) t -> p u (e t)", u=2, e=2),
                    in_=e_dram[x].rearrange("b (g u p e) t -> b g p u (e t)", g=PASSES, u=2, p=P, e=2)[
                        0, g, :, :, :
                    ],
                )

        def load_w(q):
            for e in range(2):
                for x in ("re", "im"):
                    nc.sync.dma_start(
                        out=w_raw[(x, q)][:, e, :],
                        in_=w_dram[x].rearrange("(q p e) c -> q e p c", q=PAIRS, p=P, e=2)[q, e, :, :],
                    )

        load_e(0)
        load_w(0)
        load_e(1)
        for q in range(1, PAIRS):
            load_w(q)

        e_grouped = {}
        for g in range(PASSES):
            for x in ("re", "im", "neg"):
                e_grouped[(x, g)] = keep.tile(
                    [P, PACK * POSITIONS], BF16, name="e_grp_%s%d" % (x, g), align_bytes=64
                )

        def quantise_e(x, g):
            nc.vector.quantize_mx(
                out=e_codes[x][:, g, :].bitcast(FP8X4), scales=e_scales[x][:, g, :], in_=e_grouped[(x, g)][:]
            )

        def prepare_e(g):
            for x in ("re", "im"):
                regroup(nc.vector.tensor_copy, e_grouped[(x, g)][:], e_raw[x][:, g, :, :], 0, VECTOR_POSITIONS)
                regroup(nc.scalar.copy, e_grouped[(x, g)][:], e_raw[x][:, g, :, :], VECTOR_POSITIONS, POSITIONS)
            quantise_e("re", g)
            nc.vector.tensor_scalar_mul(out=e_grouped[("neg", g)][:], in0=e_grouped[("im", g)][:], scalar1=-1.0)
            quantise_e("im", g)

        def transpose_w(q):
            grouped = []
            for e in range(2):
                words_out = keep.tile([P, 2 * BANK], F32, name="w_grp_%d%d" % (q, e), align_bytes=64)
                grouped.append(words_out)
                for xi, x in enumerate(("re", "im")):
                    words_in = w_raw[(x, q)][:, e, :].bitcast(F32)
                    bank = left_banks.tile([P, BANK], F32, name="w_bank", tag="left")
                    for gu in range(PASSES * 2):
                        nc.tensor.transpose(
                            bank[:, gu * P : (gu + 1) * P],
                            words_in[:, gu * P : (gu + 1) * P],
                            identity[:],
                        )
                    nc.scalar.copy(
                        out=words_out[:, xi * BANK : (xi + 1) * BANK].rearrange(
                            "p (g m u) -> p g m u", g=PASSES, m=P, u=2
                        ),
                        in_=bank[:].rearrange("p (g u m) -> p g m u", g=PASSES, u=2, m=P),
                    )
            return grouped

        def quantise_w(q, e, grouped):
            nc.vector.quantize_mx(
                out=w_codes[:, q, e, :].bitcast(FP8X4),
                scales=w_scales[:, q, e, :],
                in_=grouped[e][:].bitcast(BF16),
            )

        def stage1_passes(q, g, part, q_acc):
            for e in range(2):
                for xi, operand in enumerate(STAGE1_E[part]):
                    w_cols = slice((xi * PASSES + g) * P, (xi * PASSES + g + 1) * P)
                    nc.tensor.matmul_mx(
                        out=q_acc[(e, part)][:],
                        lhsT=w_codes[:, q, e, w_cols].bitcast(FP8X4),
                        lhsT_scale=w_scales[:, q, e, w_cols],
                        rhs=e_codes[operand][:, g, :].bitcast(FP8X4),
                        rhs_scale=e_scales[operand][:, g, :],
                        start=(g == 0 and xi == 0),
                        stop=(g == PASSES - 1 and xi == 1),
                    )
                if g == PASSES - 1:
                    nc.scalar.copy(out=q_raw[part][:, q, e, :], in_=q_acc[(e, part)][:])

        def quantise_q(g):
            for part in ("im", "re"):
                grouped = keep.tile([P, PACK * POSITIONS], BF16, name="q_grp_%s%d" % (part, g), align_bytes=64)
                rows = q_raw[part][:, 2 * g : 2 * g + 2, :, :].rearrange("p u e t -> p (u e) t")
                regroup(nc.vector.tensor_copy, grouped[:], rows, 0, POSITIONS)
                nc.vector.quantize_mx(
                    out=q_codes[part][:, g, :].bitcast(FP8X4), scales=q_scales[part][:, g, :], in_=grouped[:]
                )

        prepare_e(0)
        w_grouped = transpose_w(0)
        quantise_w(0, 0, w_grouped)
        quantise_e("neg", 0)
        quantise_w(0, 1, w_grouped)
        prepare_e(1)
        quantise_e("neg", 1)
        for q in range(PAIRS):
            q_acc = {}
            for part in ("im", "re"):
                for e in range(2):
                    q_acc[(e, part)] = right_banks.tile([P, BANK], F32, name="q_acc", tag="right")
            stage1_passes(q, 0, "im", q_acc)
            if q + 1 < PAIRS:
                w_grouped = transpose_w(q + 1)
                quantise_w(q + 1, 0, w_grouped)
                quantise_w(q + 1, 1, w_grouped)
            stage1_passes(q, 0, "re", q_acc)
            stage1_passes(q, 1, "im", q_acc)
            stage1_passes(q, 1, "re", q_acc)
            if q % 2 == 1:
                quantise_q(q // 2)

        s_banks = {"re": (left_banks, "left"), "im": (right_banks, "right")}
        s_acc = {}
        for g in range(PASSES):
            for part in ("re", "im"):
                for i in range(POSITION_TILES):
                    if g == 0:
                        pool, tag = s_banks[part]
                        s_acc[(part, i)] = pool.tile([P, BANK], F32, name="s_acc", tag=tag)
                    rows = slice(i * P, (i + 1) * P)
                    for n, (operand, q_part) in enumerate(STAGE2_TERMS[part]):
                        nc.tensor.matmul_mx(
                            out=s_acc[(part, i)][:],
                            lhsT=e_codes[operand][:, g, rows].bitcast(FP8X4),
                            lhsT_scale=e_scales[operand][:, g, rows],
                            rhs=q_codes[q_part][:, g, :].bitcast(FP8X4),
                            rhs_scale=q_scales[q_part][:, g, :],
                            start=(g == 0 and n == 0),
                            stop=(g == PASSES - 1 and n == 1),
                        )
                    if g == PASSES - 1:
                        s_sb = keep.tile([P, POSITIONS], F32, name="s_sb_%s%d" % (part, i))
                        if i % 2 == 0:
                            nc.scalar.copy(out=s_sb[:], in_=s_acc[(part, i)][:])
                        else:
                            nc.vector.tensor_copy(out=s_sb[:], in_=s_acc[(part, i)][:])
                        nc.sync.dma_start(out=s_dram[part][0, rows, :], in_=s_sb[:])
